import numpy as np
import ml_dtypes


def mxq(x, axis, fmt="e4m3"):
    dtype, down = {"e4m3": (ml_dtypes.float8_e4m3fn, 7), "e5m2": (ml_dtypes.float8_e5m2, 14)}[fmt]
    v = np.moveaxis(np.asarray(x, np.float32).astype(ml_dtypes.bfloat16).astype(np.float64), axis, -1)
    blocks = v.reshape(v.shape[:-1] + (-1, 32))
    amax = np.abs(blocks).max(-1, keepdims=True)
    byte = np.maximum(np.where(amax > 0, np.frexp(amax)[1] - 1 + 127, 0) - down, 1)
    scale = np.exp2(byte - 127.0)
    codes = (blocks / scale).astype(np.float32).astype(dtype).astype(np.float64)
    return np.moveaxis((codes * scale).reshape(v.shape), -1, axis)


WIDE = False


def mx_kscale(k):
    if not WIDE:
        return np.ones(k)
    levels = np.array([10, -10, 5, -5, 0])
    a = np.random.permutation(np.resize(levels, k // 512 * 4)).reshape(k // 512, 4)
    idx = np.arange(k)
    return np.exp2(a[idx // 512, idx % 128 // 32])


BF16 = ml_dtypes.bfloat16


def bf(x):
    return np.asarray(x, np.float32).astype(BF16)


def f64(x):
    return np.asarray(x).astype(np.float64)


B, S, DIM, N_HEADS, Q_LORA, KV_LORA, NOPE, ROPE, V_HEAD = 1, 512, 2048, 16, 1536, 512, 128, 64, 128
HV = N_HEADS * V_HEAD


def setup_inputs():
    s, t = mx_kscale(KV_LORA), mx_kscale(HV)
    return {"o_lat": bf(np.random.standard_normal((B, S, N_HEADS, KV_LORA)) * 0.35 * s),
            "w_uv": bf(np.random.standard_normal((N_HEADS, V_HEAD, KV_LORA)) * 2.0 / np.sqrt(KV_LORA) / s * t.reshape(N_HEADS, V_HEAD, 1)),
            "wo": bf(np.random.standard_normal((DIM, HV)) / np.sqrt(HV) / t)}


def reference(o_lat, w_uv, wo):
    ol = mxq(f64(o_lat), 3, "e4m3").transpose(0, 2, 1, 3)
    wv = mxq(f64(w_uv), 2, "e4m3").transpose(0, 2, 1)
    o = ol @ wv[None]
    o = o.transpose(0, 2, 1, 3).reshape(B, S, HV)
    return mxq(o, 2, "e4m3") @ mxq(f64(wo), 1, "e4m3").T

@@ -1,0 +1,241 @@
+from contextlib import ExitStack
+
+import concourse.masks as masks
+import concourse.mybir as mybir
+
+BF16 = mybir.dt.bfloat16
+F32 = mybir.dt.float32
+I32 = mybir.dt.int32
+U32 = mybir.dt.uint32
+U8 = mybir.dt.uint8
+FP8X4 = mybir.dt.float8_e4m3fn_x4
+
+P = 128
+S = 512
+HEADS = 16
+LATENT = 512
+V_HEAD = 128
+HV = HEADS * V_HEAD
+DIM = 2048
+
+FLOPS = 2 * S * HEADS * V_HEAD * LATENT + 2 * S * HV * DIM
+
+K_PASS = 512
+PAIRS = K_PASS // 2
+PIECE_COLS = 4096
+PIECE_PASSES = PIECE_COLS // K_PASS
+BANK_PASSES = 2
+S_TILES = S // P
+K_GROUPS = HV // K_PASS
+N_CHUNK = 512
+HALF = P // 2
+
+W_PIECES = HEADS * V_HEAD * LATENT // (P * PIECE_COLS)
+O_PIECES = S * HEADS * LATENT // (P * PIECE_COLS)
+X_PIECES = DIM * HV // (P * PIECE_COLS)
+RAW_BUFS = 8
+
+
+def tile_mla_pc_kernel(tc, o_lat, w_uv, wo, out):
+    nc = tc.nc
+    with ExitStack() as ctx:
+        ctx.enter_context(tc.manual_schedule())
+        keep = ctx.enter_context(tc.tile_pool(name="keep", bufs=1))
+        raw_pool = ctx.enter_context(tc.tile_pool(name="raw", bufs=RAW_BUFS))
+        grouped_pool = ctx.enter_context(tc.tile_pool(name="grouped", bufs=3))
+        ol_pool = ctx.enter_context(tc.tile_pool(name="ol", bufs=3))
+        og_pool = ctx.enter_context(tc.tile_pool(name="og", bufs=3))
+        x_pool = ctx.enter_context(tc.tile_pool(name="x", bufs=2))
+        out_pool = ctx.enter_context(tc.tile_pool(name="outs", bufs=6))
+        flip_psum = ctx.enter_context(tc.psum_pool(name="flip", bufs=4))
+        acc_psum = ctx.enter_context(tc.psum_pool(name="acc", bufs=4))
+
+        ident = keep.tile([P, P], F32)
+        masks.make_identity(nc, ident[:])
+
+        w_codes = keep.tile([P, HEADS, 3 * HALF], U32, align_bytes=64)
+        w_scales = keep.tile([P, HEADS, 3 * HALF], U8, align_bytes=64)
+        nc.vector.memset(w_codes[:, :, HALF : 2 * HALF].bitcast(I32), 0)
+        nc.vector.memset(w_scales[:, :, HALF : 2 * HALF].bitcast(I32), 0)
+
+        o_codes = keep.tile([P, S_TILES, K_GROUPS, P], U32, align_bytes=64)
+        o_scales = keep.tile([P, S_TILES, K_GROUPS, P], U8, align_bytes=64)
+
+        pieces = (
+            [("w_uv", i) for i in range(W_PIECES)]
+            + [("o_lat", i) for i in range(O_PIECES)]
+            + [("wo", i) for i in range(X_PIECES)]
+        )
+        raw_of = {}
+        grouped_of = {}
+        ol_of = {}
+        og_of = {}
+        x_of = {}
+
+        def load(j):
+            kind, i = pieces[j]
+            raw = raw_pool.tile([P, PIECE_COLS], BF16)
+            if kind == "w_uv":
+                rows = w_uv.rearrange("h d c -> (h d c)").rearrange(
+                    "(q m x) -> m q x", m=P, x=2 * LATENT
+                )
+                nc.sync.dma_start(
+                    out=raw[:].rearrange("m (q x) -> m q x", x=2 * LATENT),
+                    in_=rows[:, 4 * i : 4 * i + 4, :],
+                )
+            elif kind == "o_lat":
+                tok, half = divmod(i, 2)
+                nc.sync.dma_start(
+                    out=raw[:],
+                    in_=o_lat[0, tok * P : (tok + 1) * P, 8 * half : 8 * half + 8, :].rearrange(
+                        "s h c -> s (h c)"
+                    ),
+                )
+            else:
+                nc.sync.dma_start(
+                    out=raw[:].rearrange("p (j k) -> p j k", j=2),
+                    in_=wo[2 * i * P : (2 * i + 2) * P, :].rearrange("(j p) k -> p j k", p=P),
+                )
+            raw_of[j] = raw
+
+        def flip(j):
+            kind, i = pieces[j]
+            pairs = raw_of[j][:].bitcast(F32)
+            grouped = grouped_pool.tile([P, PIECE_COLS], BF16, align_bytes=64)
+            grouped_pairs = grouped[:].bitcast(F32).rearrange(
+                "p (a r u) -> p a r u", a=PIECE_PASSES, u=2
+            )
+            for b in range(PIECE_PASSES // BANK_PASSES):
+                bank = flip_psum.tile([P, BANK_PASSES, 2, P], F32)
+                for a in range(BANK_PASSES):
+                    if kind == "wo":
+                        first = a * (HV // 2) + b * PAIRS
+                    else:
+                        first = (b * BANK_PASSES + a) * PAIRS
+                    for u in range(2):
+                        nc.tensor.transpose(
+                            bank[:, a, u, :],
+                            pairs[:, first + u * P : first + (u + 1) * P],
+                            ident[:],
+                        )
+                src = bank[:].rearrange("p a u r -> p a r u")
+                dst = grouped_pairs[:, b * BANK_PASSES : (b + 1) * BANK_PASSES, :, :]
+                if b % 2 == 0:
+                    nc.vector.tensor_copy(out=dst, in_=src)
+                else:
+                    nc.scalar.copy(out=dst, in_=src)
+            grouped_of[j] = grouped
+
+        def quantise(j):
+            kind, i = pieces[j]
+            grouped = grouped_of[j]
+            if kind == "w_uv":
+                for a in range(PIECE_PASSES):
+                    for side in range(2):
+                        first = (a * P + side * HALF) * 4
+                        cols = slice(2 * side * HALF, (2 * side + 1) * HALF)
+                        nc.vector.quantize_mx(
+                            out=w_codes[:, PIECE_PASSES * i + a, cols].bitcast(FP8X4),
+                            scales=w_scales[:, PIECE_PASSES * i + a, cols],
+                            in_=grouped[:, first : first + 4 * HALF],
+                        )
+            elif kind == "o_lat":
+                ol_codes = ol_pool.tile([P, PIECE_PASSES, P], U32, align_bytes=64)
+                ol_scales = ol_pool.tile([P, PIECE_PASSES, P], U8, align_bytes=64)
+                for gg in range(2):
+                    heads = slice(4 * gg, 4 * gg + 4)
+                    nc.vector.quantize_mx(
+                        out=ol_codes[:, heads, :].rearrange("p h s -> p (h s)").bitcast(FP8X4),
+                        scales=ol_scales[:, heads, :].rearrange("p h s -> p (h s)"),
+                        in_=grouped[:, gg * PIECE_COLS // 2 : (gg + 1) * PIECE_COLS // 2],
+                    )
+                ol_of[j] = (ol_codes, ol_scales)
+            else:
+                chunk, part = divmod(i, 2)
+                if part == 0:
+                    x_codes = x_pool.tile([P, K_GROUPS, N_CHUNK], U32, align_bytes=64)
+                    x_scales = x_pool.tile([P, K_GROUPS, N_CHUNK], U8, align_bytes=64)
+                    x_of[chunk] = (x_codes, x_scales)
+                x_codes, x_scales = x_of[chunk]
+                cols = slice(part * 2 * P, (part + 1) * 2 * P)
+                for g in range(K_GROUPS):
+                    nc.vector.quantize_mx(
+                        out=x_codes[:, g, cols].bitcast(FP8X4),
+                        scales=x_scales[:, g, cols],
+                        in_=grouped[:, g * 8 * P : (g + 1) * 8 * P],
+                    )
+
+        def up_project(j):
+            kind, i = pieces[j]
+            tok, half = divmod(i, 2)
+            ol_codes, ol_scales = ol_of[j]
+            o_grouped = og_pool.tile([P, 2, P, 4], BF16, align_bytes=64)
+            for gg in range(2):
+                o_bank = acc_psum.tile([P, 4, P], F32, tag="acc")
+                for t in range(4):
+                    plane = 4 * (2 * half + gg) + t
+                    for side in range(2):
+                        cols = slice(side * HALF, side * HALF + P)
+                        head = 4 * gg + 2 * (t // 2) + side
+                        nc.tensor.matmul_mx(
+                            out=o_bank[:, t, :],
+                            lhsT=w_codes[:, plane, cols].bitcast(FP8X4),
+                            lhsT_scale=w_scales[:, plane, cols],
+                            rhs=ol_codes[:, head, :].bitcast(FP8X4),
+                            rhs_scale=ol_scales[:, head, :],
+                            start=(side == 0),
+                            stop=(side == 1),
+                        )
+                nc.scalar.copy(
+                    out=o_grouped[:, gg, :, :], in_=o_bank[:].rearrange("p t s -> p s t")
+                )
+            og_of[j] = o_grouped
+
+        def quantise_o(j):
+            kind, i = pieces[j]
+            tok, half = divmod(i, 2)
+            groups = slice(2 * half, 2 * half + 2)
+            nc.vector.quantize_mx(
+                out=o_codes[:, tok, groups, :].rearrange("p g s -> p (g s)").bitcast(FP8X4),
+                scales=o_scales[:, tok, groups, :].rearrange("p g s -> p (g s)"),
+                in_=og_of[j][:].rearrange("p g s t -> p (g s t)"),
+            )
+
+        def project_out(chunk):
+            x_codes, x_scales = x_of[chunk]
+            for tok in range(S_TILES):
+                out_bank = acc_psum.tile([P, N_CHUNK], F32, tag="acc")
+                for g in range(K_GROUPS):
+                    nc.tensor.matmul_mx(
+                        out=out_bank[:],
+                        lhsT=o_codes[:, tok, g, :].bitcast(FP8X4),
+                        lhsT_scale=o_scales[:, tok, g, :],
+                        rhs=x_codes[:, g, :].bitcast(FP8X4),
+                        rhs_scale=x_scales[:, g, :],
+                        start=(g == 0),
+                        stop=(g == K_GROUPS - 1),
+                    )
+                result = out_pool.tile([P, N_CHUNK], F32)
+                nc.scalar.copy(out=result[:], in_=out_bank[:])
+                nc.sync.dma_start(
+                    out=out[0, tok * P : (tok + 1) * P, chunk * N_CHUNK : (chunk + 1) * N_CHUNK],
+                    in_=result[:],
+                )
+
+        for j in range(RAW_BUFS):
+            load(j)
+        for j in range(len(pieces) + 2):
+            if j < len(pieces):
+                flip(j)
+                if j + RAW_BUFS < len(pieces):
+                    load(j + RAW_BUFS)
+            if 0 <= j - 1 < len(pieces):
+                quantise(j - 1)
+            if 0 <= j - 3 < len(pieces) and pieces[j - 3][0] == "o_lat":
+                quantise_o(j - 3)
+            if 0 <= j - 2 < len(pieces):
+                kind, i = pieces[j - 2]
+                if kind == "o_lat":
+                    up_project(j - 2)
+                if kind == "wo" and i % 2 == 1:
+                    project_out(i // 2)

@@ -47,8 +47,8 @@ def tile_mla_pc_kernel(tc, o_lat, w_uv, wo, out):
         og_pool = ctx.enter_context(tc.tile_pool(name="og", bufs=3))
         x_pool = ctx.enter_context(tc.tile_pool(name="x", bufs=2))
         out_pool = ctx.enter_context(tc.tile_pool(name="outs", bufs=6))
-        flip_psum = ctx.enter_context(tc.psum_pool(name="flip", bufs=4))
-        acc_psum = ctx.enter_context(tc.psum_pool(name="acc", bufs=4))
+        flip_psum = ctx.enter_context(tc.psum_pool(name="flip", bufs=5))
+        acc_psum = ctx.enter_context(tc.psum_pool(name="acc", bufs=3))
 
         ident = keep.tile([P, P], F32)
         masks.make_identity(nc, ident[:])
@@ -120,7 +120,7 @@ def tile_mla_pc_kernel(tc, o_lat, w_uv, wo, out):
                         )
                 src = bank[:].rearrange("p a u r -> p a r u")
                 dst = grouped_pairs[:, b * BANK_PASSES : (b + 1) * BANK_PASSES, :, :]
-                if b % 2 == 0:
+                if b == 0:
                     nc.vector.tensor_copy(out=dst, in_=src)
                 else:
                     nc.scalar.copy(out=dst, in_=src)
@@ -186,9 +186,11 @@ def tile_mla_pc_kernel(tc, o_lat, w_uv, wo, out):
                             start=(side == 0),
                             stop=(side == 1),
                         )
-                nc.scalar.copy(
-                    out=o_grouped[:, gg, :, :], in_=o_bank[:].rearrange("p t s -> p s t")
-                )
+                planes = o_bank[:].rearrange("p t s -> p s t")
+                if gg == 0:
+                    nc.vector.tensor_copy(out=o_grouped[:, gg, :, :], in_=planes)
+                else:
+                    nc.scalar.copy(out=o_grouped[:, gg, :, :], in_=planes)
             og_of[j] = o_grouped
 
         def quantise_o(j):

@@ -31,7 +31,6 @@ N_CHUNK = 512
 HALF = P // 2
 
 W_PIECES = HEADS * V_HEAD * LATENT // (P * PIECE_COLS)
-O_PIECES = S * HEADS * LATENT // (P * PIECE_COLS)
 X_PIECES = DIM * HV // (P * PIECE_COLS)
 RAW_BUFS = 8
 
@@ -61,11 +60,11 @@ def tile_mla_pc_kernel(tc, o_lat, w_uv, wo, out):
         o_codes = keep.tile([P, S_TILES, K_GROUPS, P], U32, align_bytes=64)
         o_scales = keep.tile([P, S_TILES, K_GROUPS, P], U8, align_bytes=64)
 
-        pieces = (
-            [("w_uv", i) for i in range(W_PIECES)]
-            + [("o_lat", i) for i in range(O_PIECES)]
-            + [("wo", i) for i in range(X_PIECES)]
-        )
+        pieces = []
+        for half in range(W_PIECES):
+            pieces.append(("w_uv", half))
+            pieces.extend([("o_lat", (tok, half)) for tok in range(S_TILES)])
+        pieces.extend([("wo", i) for i in range(X_PIECES)])
         raw_of = {}
         grouped_of = {}
         ol_of = {}
@@ -84,7 +83,7 @@ def tile_mla_pc_kernel(tc, o_lat, w_uv, wo, out):
                     in_=rows[:, 4 * i : 4 * i + 4, :],
                 )
             elif kind == "o_lat":
-                tok, half = divmod(i, 2)
+                tok, half = i
                 nc.sync.dma_start(
                     out=raw[:],
                     in_=o_lat[0, tok * P : (tok + 1) * P, 8 * half : 8 * half + 8, :].rearrange(
@@ -99,7 +98,7 @@ def tile_mla_pc_kernel(tc, o_lat, w_uv, wo, out):
             raw_of[j] = raw
 
         def flip(j):
-            kind, i = pieces[j]
+            kind = pieces[j][0]
             pairs = raw_of[j][:].bitcast(F32)
             grouped = grouped_pool.tile([P, PIECE_COLS], BF16, align_bytes=64)
             grouped_pairs = grouped[:].bitcast(F32).rearrange(
@@ -166,8 +165,7 @@ def tile_mla_pc_kernel(tc, o_lat, w_uv, wo, out):
                     )
 
         def up_project(j):
-            kind, i = pieces[j]
-            tok, half = divmod(i, 2)
+            tok, half = pieces[j][1]
             ol_codes, ol_scales = ol_of[j]
             o_grouped = og_pool.tile([P, 2, P, 4], BF16, align_bytes=64)
             for gg in range(2):
@@ -186,16 +184,13 @@ def tile_mla_pc_kernel(tc, o_lat, w_uv, wo, out):
                             start=(side == 0),
                             stop=(side == 1),
                         )
-                planes = o_bank[:].rearrange("p t s -> p s t")
-                if gg == 0:
-                    nc.vector.tensor_copy(out=o_grouped[:, gg, :, :], in_=planes)
-                else:
-                    nc.scalar.copy(out=o_grouped[:, gg, :, :], in_=planes)
+                nc.scalar.copy(
+                    out=o_grouped[:, gg, :, :], in_=o_bank[:].rearrange("p t s -> p s t")
+                )
             og_of[j] = o_grouped
 
         def quantise_o(j):
-            kind, i = pieces[j]
-            tok, half = divmod(i, 2)
+            tok, half = pieces[j][1]
             groups = slice(2 * half, 2 * half + 2)
             nc.vector.quantize_mx(
                 out=o_codes[:, tok, groups, :].rearrange("p g s -> p (g s)").bitcast(FP8X4),

from contextlib import ExitStack

import concourse.masks as masks
import concourse.mybir as mybir

BF16 = mybir.dt.bfloat16
F32 = mybir.dt.float32
I32 = mybir.dt.int32
U32 = mybir.dt.uint32
U8 = mybir.dt.uint8
FP8X4 = mybir.dt.float8_e4m3fn_x4

P = 128
S = 512
HEADS = 16
LATENT = 512
V_HEAD = 128
HV = HEADS * V_HEAD
DIM = 2048

FLOPS = 2 * S * HEADS * V_HEAD * LATENT + 2 * S * HV * DIM

K_PASS = 512
PAIRS = K_PASS // 2
PIECE_COLS = 4096
PIECE_PASSES = PIECE_COLS // K_PASS
BANK_PASSES = 2
S_TILES = S // P
K_GROUPS = HV // K_PASS
N_CHUNK = 512
HALF = P // 2

W_PIECES = HEADS * V_HEAD * LATENT // (P * PIECE_COLS)
X_PIECES = DIM * HV // (P * PIECE_COLS)
RAW_BUFS = 8


def tile_mla_pc_kernel(tc, o_lat, w_uv, wo, out):
    nc = tc.nc
    with ExitStack() as ctx:
        ctx.enter_context(tc.manual_schedule())
        keep = ctx.enter_context(tc.tile_pool(name="keep", bufs=1))
        raw_pool = ctx.enter_context(tc.tile_pool(name="raw", bufs=RAW_BUFS))
        grouped_pool = ctx.enter_context(tc.tile_pool(name="grouped", bufs=3))
        ol_pool = ctx.enter_context(tc.tile_pool(name="ol", bufs=3))
        og_pool = ctx.enter_context(tc.tile_pool(name="og", bufs=3))
        x_pool = ctx.enter_context(tc.tile_pool(name="x", bufs=2))
        out_pool = ctx.enter_context(tc.tile_pool(name="outs", bufs=6))
        flip_psum = ctx.enter_context(tc.psum_pool(name="flip", bufs=5))
        acc_psum = ctx.enter_context(tc.psum_pool(name="acc", bufs=3))

        ident = keep.tile([P, P], F32)
        masks.make_identity(nc, ident[:])

        w_codes = keep.tile([P, HEADS, 3 * HALF], U32, align_bytes=64)
        w_scales = keep.tile([P, HEADS, 3 * HALF], U8, align_bytes=64)
        nc.vector.memset(w_codes[:, :, HALF : 2 * HALF].bitcast(I32), 0)
        nc.vector.memset(w_scales[:, :, HALF : 2 * HALF].bitcast(I32), 0)

        o_codes = keep.tile([P, S_TILES, K_GROUPS, P], U32, align_bytes=64)
        o_scales = keep.tile([P, S_TILES, K_GROUPS, P], U8, align_bytes=64)

        pieces = []
        for half in range(W_PIECES):
            pieces.append(("w_uv", half))
            pieces.extend([("o_lat", (tok, half)) for tok in range(S_TILES)])
        pieces.extend([("wo", i) for i in range(X_PIECES)])
        raw_of = {}
        grouped_of = {}
        ol_of = {}
        og_of = {}
        x_of = {}

        def load(j):
            kind, i = pieces[j]
            raw = raw_pool.tile([P, PIECE_COLS], BF16)
            if kind == "w_uv":
                rows = w_uv.rearrange("h d c -> (h d c)").rearrange(
                    "(q m x) -> m q x", m=P, x=2 * LATENT
                )
                nc.sync.dma_start(
                    out=raw[:].rearrange("m (q x) -> m q x", x=2 * LATENT),
                    in_=rows[:, 4 * i : 4 * i + 4, :],
                )
            elif kind == "o_lat":
                tok, half = i
                nc.sync.dma_start(
                    out=raw[:],
                    in_=o_lat[0, tok * P : (tok + 1) * P, 8 * half : 8 * half + 8, :].rearrange(
                        "s h c -> s (h c)"
                    ),
                )
            else:
                nc.sync.dma_start(
                    out=raw[:].rearrange("p (j k) -> p j k", j=2),
                    in_=wo[2 * i * P : (2 * i + 2) * P, :].rearrange("(j p) k -> p j k", p=P),
                )
            raw_of[j] = raw

        def flip(j):
            kind = pieces[j][0]
            pairs = raw_of[j][:].bitcast(F32)
            grouped = grouped_pool.tile([P, PIECE_COLS], BF16, align_bytes=64)
            grouped_pairs = grouped[:].bitcast(F32).rearrange(
                "p (a r u) -> p a r u", a=PIECE_PASSES, u=2
            )
            for b in range(PIECE_PASSES // BANK_PASSES):
                bank = flip_psum.tile([P, BANK_PASSES, 2, P], F32)
                for a in range(BANK_PASSES):
                    if kind == "wo":
                        first = a * (HV // 2) + b * PAIRS
                    else:
                        first = (b * BANK_PASSES + a) * PAIRS
                    for u in range(2):
                        nc.tensor.transpose(
                            bank[:, a, u, :],
                            pairs[:, first + u * P : first + (u + 1) * P],
                            ident[:],
                        )
                src = bank[:].rearrange("p a u r -> p a r u")
                dst = grouped_pairs[:, b * BANK_PASSES : (b + 1) * BANK_PASSES, :, :]
                if b == 0:
                    nc.vector.tensor_copy(out=dst, in_=src)
                else:
                    nc.scalar.copy(out=dst, in_=src)
            grouped_of[j] = grouped

        def quantise(j):
            kind, i = pieces[j]
            grouped = grouped_of[j]
            if kind == "w_uv":
                for a in range(PIECE_PASSES):
                    for side in range(2):
                        first = (a * P + side * HALF) * 4
                        cols = slice(2 * side * HALF, (2 * side + 1) * HALF)
                        nc.vector.quantize_mx(
                            out=w_codes[:, PIECE_PASSES * i + a, cols].bitcast(FP8X4),
                            scales=w_scales[:, PIECE_PASSES * i + a, cols],
                            in_=grouped[:, first : first + 4 * HALF],
                        )
            elif kind == "o_lat":
                ol_codes = ol_pool.tile([P, PIECE_PASSES, P], U32, align_bytes=64)
                ol_scales = ol_pool.tile([P, PIECE_PASSES, P], U8, align_bytes=64)
                for gg in range(2):
                    heads = slice(4 * gg, 4 * gg + 4)
                    nc.vector.quantize_mx(
                        out=ol_codes[:, heads, :].rearrange("p h s -> p (h s)").bitcast(FP8X4),
                        scales=ol_scales[:, heads, :].rearrange("p h s -> p (h s)"),
                        in_=grouped[:, gg * PIECE_COLS // 2 : (gg + 1) * PIECE_COLS // 2],
                    )
                ol_of[j] = (ol_codes, ol_scales)
            else:
                chunk, part = divmod(i, 2)
                if part == 0:
                    x_codes = x_pool.tile([P, K_GROUPS, N_CHUNK], U32, align_bytes=64)
                    x_scales = x_pool.tile([P, K_GROUPS, N_CHUNK], U8, align_bytes=64)
                    x_of[chunk] = (x_codes, x_scales)
                x_codes, x_scales = x_of[chunk]
                cols = slice(part * 2 * P, (part + 1) * 2 * P)
                for g in range(K_GROUPS):
                    nc.vector.quantize_mx(
                        out=x_codes[:, g, cols].bitcast(FP8X4),
                        scales=x_scales[:, g, cols],
                        in_=grouped[:, g * 8 * P : (g + 1) * 8 * P],
                    )

        def up_project(j):
            tok, half = pieces[j][1]
            ol_codes, ol_scales = ol_of[j]
            o_grouped = og_pool.tile([P, 2, P, 4], BF16, align_bytes=64)
            for gg in range(2):
                o_bank = acc_psum.tile([P, 4, P], F32, tag="acc")
                for t in range(4):
                    plane = 4 * (2 * half + gg) + t
                    for side in range(2):
                        cols = slice(side * HALF, side * HALF + P)
                        head = 4 * gg + 2 * (t // 2) + side
                        nc.tensor.matmul_mx(
                            out=o_bank[:, t, :],
                            lhsT=w_codes[:, plane, cols].bitcast(FP8X4),
                            lhsT_scale=w_scales[:, plane, cols],
                            rhs=ol_codes[:, head, :].bitcast(FP8X4),
                            rhs_scale=ol_scales[:, head, :],
                            start=(side == 0),
                            stop=(side == 1),
                        )
                nc.scalar.copy(
                    out=o_grouped[:, gg, :, :], in_=o_bank[:].rearrange("p t s -> p s t")
                )
            og_of[j] = o_grouped

        def quantise_o(j):
            tok, half = pieces[j][1]
            groups = slice(2 * half, 2 * half + 2)
            nc.vector.quantize_mx(
                out=o_codes[:, tok, groups, :].rearrange("p g s -> p (g s)").bitcast(FP8X4),
                scales=o_scales[:, tok, groups, :].rearrange("p g s -> p (g s)"),
                in_=og_of[j][:].rearrange("p g s t -> p (g s t)"),
            )

        def project_out(chunk):
            x_codes, x_scales = x_of[chunk]
            for tok in range(S_TILES):
                out_bank = acc_psum.tile([P, N_CHUNK], F32, tag="acc")
                for g in range(K_GROUPS):
                    nc.tensor.matmul_mx(
                        out=out_bank[:],
                        lhsT=o_codes[:, tok, g, :].bitcast(FP8X4),
                        lhsT_scale=o_scales[:, tok, g, :],
                        rhs=x_codes[:, g, :].bitcast(FP8X4),
                        rhs_scale=x_scales[:, g, :],
                        start=(g == 0),
                        stop=(g == K_GROUPS - 1),
                    )
                result = out_pool.tile([P, N_CHUNK], F32)
                nc.scalar.copy(out=result[:], in_=out_bank[:])
                nc.sync.dma_start(
                    out=out[0, tok * P : (tok + 1) * P, chunk * N_CHUNK : (chunk + 1) * N_CHUNK],
                    in_=result[:],
                )

        for j in range(RAW_BUFS):
            load(j)
        for j in range(len(pieces) + 2):
            if j < len(pieces):
                flip(j)
                if j + RAW_BUFS < len(pieces):
                    load(j + RAW_BUFS)
            if 0 <= j - 1 < len(pieces):
                quantise(j - 1)
            if 0 <= j - 3 < len(pieces) and pieces[j - 3][0] == "o_lat":
                quantise_o(j - 3)
            if 0 <= j - 2 < len(pieces):
                kind, i = pieces[j - 2]
                if kind == "o_lat":
                    up_project(j - 2)
                if kind == "wo" and i % 2 == 1:
                    project_out(i // 2)
